import numpy as np
import ml_dtypes

BF16 = ml_dtypes.bfloat16


def bf(x):
    return np.asarray(x, np.float32).astype(BF16)


def f32(x):
    return np.asarray(x, np.float32)


def f64(x):
    return np.asarray(x).astype(np.float64)


def striped(idx):
    return np.tile(idx.reshape(-1, 16).T, (8, 1))


E, S, M, F, K, A, N = 128, 512, 128, 128, 4, 512, 2048


def setup_inputs():
    return {"table": bf(np.random.standard_normal((E, S))), "w": bf(np.random.standard_normal((E, M)) * np.sqrt(K / E)), "b1": f32(0.1 * np.random.standard_normal((M, 1))), "w2": bf(np.random.standard_normal((M, F)) * np.sqrt(2.0 / M)), "b2": f32(0.1 * np.random.standard_normal((F, 1))), "w3": bf(np.random.standard_normal((F, 1)) * np.sqrt(2.0 / F)), "b3": f32(0.5 + 0.1 * np.random.standard_normal((1, 1))), "offs": striped(np.concatenate([np.random.permutation(S) for _ in range(K)]))}


def reference(table, w, b1, w2, b2, w3, b3, offs):
    idx = offs[:16].T.reshape(-1)
    p = f64(w).T @ f64(table)[:, idx]
    r = p.reshape(M, K, A).sum(axis=1) / K
    h1 = np.maximum(r + f64(b1), 0.0)
    h2 = np.maximum(f64(w2).T @ h1 + f64(b2), 0.0)
    return f64(w3).T @ h2 + f64(b3)

@@ -1,0 +1,62 @@
+import concourse.mybir as mybir
+
+BF16, F32, U16 = mybir.dt.bfloat16, mybir.dt.float32, mybir.dt.uint16
+RELU = mybir.ActivationFunctionType.Relu
+IDENTITY = mybir.ActivationFunctionType.Identity
+
+E, S, M, F = 128, 512, 128, 128
+CARDS, ACTIONS = 4, 512
+N = CARDS * ACTIONS
+HALVES = 2
+WIDTH = ACTIONS // HALVES
+PER_COLUMN = 16
+
+FLOPS = 2 * E * M * N + 2 * M * F * ACTIONS + 2 * F * ACTIONS
+
+
+def tile_cardawarepolicy_kernel(tc, table, w, b1, w2, b2, w3, b3, offs, out):
+    nc = tc.nc
+    with (
+        tc.tile_pool(name="held", bufs=1) as held,
+        tc.psum_pool(name="psum", bufs=1) as psum,
+    ):
+        offsets = held.tile([128, N // PER_COLUMN], U16, name="offsets")
+        nc.sync.dma_start(offsets[:], offs)
+        cards = held.tile([E, S], BF16, name="cards")
+        nc.scalar.dma_start(cards[:], table)
+        w_sb = held.tile([E, M], BF16, name="w_sb")
+        nc.sync.dma_start(w_sb[:], w)
+        b1_sb = held.tile([M, 1], F32, name="b1_sb")
+        nc.sync.dma_start(b1_sb[:], b1)
+        w2_sb = held.tile([M, F], BF16, name="w2_sb")
+        nc.scalar.dma_start(w2_sb[:], w2)
+        b2_sb = held.tile([F, 1], F32, name="b2_sb")
+        nc.sync.dma_start(b2_sb[:], b2)
+        w3_sb = held.tile([F, 1], BF16, name="w3_sb")
+        nc.scalar.dma_start(w3_sb[:], w3)
+        b3_sb = held.tile([1, 1], F32, name="b3_sb")
+        nc.sync.dma_start(b3_sb[:], b3)
+
+        sums = [psum.tile([M, WIDTH], F32, name=f"sums{h}") for h in range(HALVES)]
+        for h in range(HALVES):
+            for card in range(CARDS):
+                first = (card * ACTIONS + h * WIDTH) // PER_COLUMN
+                picked = cards[:].indirect(offsets[:, first : first + WIDTH // PER_COLUMN])
+                nc.tensor.matmul(sums[h][:], w_sb[:], picked, start=(card == 0), stop=(card == CARDS - 1))
+
+        h1 = [held.tile([M, WIDTH], BF16, name=f"h1_{h}") for h in range(HALVES)]
+        for h in range(HALVES):
+            nc.scalar.activation(h1[h][:], sums[h][:], RELU, bias=b1_sb[:], scale=1.0 / CARDS)
+
+        layer2 = [psum.tile([F, WIDTH], F32, name=f"layer2_{h}") for h in range(HALVES)]
+        h2 = [held.tile([F, WIDTH], BF16, name=f"h2_{h}") for h in range(HALVES)]
+        for h in range(HALVES):
+            nc.tensor.matmul(layer2[h][:], w2_sb[:], h1[h][:], start=True, stop=True)
+            nc.scalar.activation(h2[h][:], layer2[h][:], RELU, bias=b2_sb[:])
+
+        layer3 = [psum.tile([1, WIDTH], F32, name=f"layer3_{h}") for h in range(HALVES)]
+        scores = [held.tile([1, WIDTH], F32, name=f"scores{h}") for h in range(HALVES)]
+        for h in range(HALVES):
+            nc.tensor.matmul(layer3[h][:], w3_sb[:], h2[h][:], start=True, stop=True)
+            nc.scalar.activation(scores[h][:], layer3[h][:], IDENTITY, bias=b3_sb[:])
+            nc.sync.dma_start(out[:, h * WIDTH : (h + 1) * WIDTH], scores[h][:])

@@ -10,6 +10,8 @@ N = CARDS * ACTIONS
 HALVES = 2
 WIDTH = ACTIONS // HALVES
 PER_COLUMN = 16
+BANK = 512
+WARM_UP = 5
 
 FLOPS = 2 * E * M * N + 2 * M * F * ACTIONS + 2 * F * ACTIONS
 
@@ -36,6 +38,12 @@ def tile_cardawarepolicy_kernel(tc, table, w, b1, w2, b2, w3, b3, offs, out):
         nc.scalar.dma_start(w3_sb[:], w3)
         b3_sb = held.tile([1, 1], F32, name="b3_sb")
         nc.sync.dma_start(b3_sb[:], b3)
+
+        zeros = held.tile([128, BANK], BF16, name="zeros")
+        nc.vector.memset(zeros[:], 0.0)
+        unread = psum.tile([128, BANK], F32, name="unread")
+        for step in range(WARM_UP):
+            nc.tensor.matmul(unread[:], zeros[:, 0:128], zeros[:], start=True, stop=True)
 
         sums = [psum.tile([M, WIDTH], F32, name=f"sums{h}") for h in range(HALVES)]
         for h in range(HALVES):

@@ -10,8 +10,6 @@ N = CARDS * ACTIONS
 HALVES = 2
 WIDTH = ACTIONS // HALVES
 PER_COLUMN = 16
-BANK = 512
-WARM_UP = 5
 
 FLOPS = 2 * E * M * N + 2 * M * F * ACTIONS + 2 * F * ACTIONS
 
@@ -39,11 +37,9 @@ def tile_cardawarepolicy_kernel(tc, table, w, b1, w2, b2, w3, b3, offs, out):
         b3_sb = held.tile([1, 1], F32, name="b3_sb")
         nc.sync.dma_start(b3_sb[:], b3)
 
-        zeros = held.tile([128, BANK], BF16, name="zeros")
-        nc.vector.memset(zeros[:], 0.0)
-        unread = psum.tile([128, BANK], F32, name="unread")
-        for step in range(WARM_UP):
-            nc.tensor.matmul(unread[:], zeros[:, 0:128], zeros[:], start=True, stop=True)
+        scratch = held.tile([128, 1], F32, name="scratch")
+        nc.gpsimd.memset(scratch[:], 0.0)
+        nc.scalar.activation(scratch[:], scratch[:], RELU)
 
         sums = [psum.tile([M, WIDTH], F32, name=f"sums{h}") for h in range(HALVES)]
         for h in range(HALVES):

@@ -1,8 +1,7 @@
 import concourse.mybir as mybir
 
 BF16, F32, U16 = mybir.dt.bfloat16, mybir.dt.float32, mybir.dt.uint16
-RELU = mybir.ActivationFunctionType.Relu
-IDENTITY = mybir.ActivationFunctionType.Identity
+MULT, ADD, MAX = mybir.AluOpType.mult, mybir.AluOpType.add, mybir.AluOpType.max
 
 E, S, M, F = 128, 512, 128, 128
 CARDS, ACTIONS = 4, 512
@@ -37,9 +36,10 @@ def tile_cardawarepolicy_kernel(tc, table, w, b1, w2, b2, w3, b3, offs, out):
         b3_sb = held.tile([1, 1], F32, name="b3_sb")
         nc.sync.dma_start(b3_sb[:], b3)
 
-        scratch = held.tile([128, 1], F32, name="scratch")
-        nc.gpsimd.memset(scratch[:], 0.0)
-        nc.scalar.activation(scratch[:], scratch[:], RELU)
+        b1_x4 = held.tile([M, 1], F32, name="b1_x4")
+        nc.vector.tensor_scalar_mul(b1_x4[:], b1_sb[:], float(CARDS))
+        b2_x4 = held.tile([F, 1], F32, name="b2_x4")
+        nc.vector.tensor_scalar_mul(b2_x4[:], b2_sb[:], float(CARDS))
 
         sums = [psum.tile([M, WIDTH], F32, name=f"sums{h}") for h in range(HALVES)]
         for h in range(HALVES):
@@ -48,19 +48,19 @@ def tile_cardawarepolicy_kernel(tc, table, w, b1, w2, b2, w3, b3, offs, out):
                 picked = cards[:].indirect(offsets[:, first : first + WIDTH // PER_COLUMN])
                 nc.tensor.matmul(sums[h][:], w_sb[:], picked, start=(card == 0), stop=(card == CARDS - 1))
 
-        h1 = [held.tile([M, WIDTH], BF16, name=f"h1_{h}") for h in range(HALVES)]
+        h1_x4 = [held.tile([M, WIDTH], BF16, name=f"h1_x4_{h}") for h in range(HALVES)]
         for h in range(HALVES):
-            nc.scalar.activation(h1[h][:], sums[h][:], RELU, bias=b1_sb[:], scale=1.0 / CARDS)
+            nc.vector.tensor_scalar(h1_x4[h][:], sums[h][:], b1_x4[:], 0.0, ADD, MAX)
 
         layer2 = [psum.tile([F, WIDTH], F32, name=f"layer2_{h}") for h in range(HALVES)]
-        h2 = [held.tile([F, WIDTH], BF16, name=f"h2_{h}") for h in range(HALVES)]
+        h2_x4 = [held.tile([F, WIDTH], BF16, name=f"h2_x4_{h}") for h in range(HALVES)]
         for h in range(HALVES):
-            nc.tensor.matmul(layer2[h][:], w2_sb[:], h1[h][:], start=True, stop=True)
-            nc.scalar.activation(h2[h][:], layer2[h][:], RELU, bias=b2_sb[:])
+            nc.tensor.matmul(layer2[h][:], w2_sb[:], h1_x4[h][:], start=True, stop=True)
+            nc.vector.tensor_scalar(h2_x4[h][:], layer2[h][:], b2_x4[:], 0.0, ADD, MAX)
 
         layer3 = [psum.tile([1, WIDTH], F32, name=f"layer3_{h}") for h in range(HALVES)]
         scores = [held.tile([1, WIDTH], F32, name=f"scores{h}") for h in range(HALVES)]
         for h in range(HALVES):
-            nc.tensor.matmul(layer3[h][:], w3_sb[:], h2[h][:], start=True, stop=True)
-            nc.scalar.activation(scores[h][:], layer3[h][:], IDENTITY, bias=b3_sb[:])
+            nc.tensor.matmul(layer3[h][:], w3_sb[:], h2_x4[h][:], start=True, stop=True)
+            nc.vector.tensor_scalar(scores[h][:], layer3[h][:], 1.0 / CARDS, b3_sb[:], MULT, ADD)
             nc.sync.dma_start(out[:, h * WIDTH : (h + 1) * WIDTH], scores[h][:])

@@ -9,6 +9,7 @@ N = CARDS * ACTIONS
 HALVES = 2
 WIDTH = ACTIONS // HALVES
 PER_COLUMN = 16
+WARM_UP = 14
 
 FLOPS = 2 * E * M * N + 2 * M * F * ACTIONS + 2 * F * ACTIONS
 
@@ -35,6 +36,12 @@ def tile_cardawarepolicy_kernel(tc, table, w, b1, w2, b2, w3, b3, offs, out):
         nc.scalar.dma_start(w3_sb[:], w3)
         b3_sb = held.tile([1, 1], F32, name="b3_sb")
         nc.sync.dma_start(b3_sb[:], b3)
+
+        zeros = held.tile([128, 128], BF16, name="zeros")
+        nc.vector.memset(zeros[:], 0.0)
+        unread = psum.tile([128, 128], F32, name="unread")
+        for step in range(WARM_UP):
+            nc.tensor.matmul(unread[:], zeros[:], zeros[:], start=True, stop=True)
 
         b1_x4 = held.tile([M, 1], F32, name="b1_x4")
         nc.vector.tensor_scalar_mul(b1_x4[:], b1_sb[:], float(CARDS))

@@ -9,6 +9,8 @@ N = CARDS * ACTIONS
 HALVES = 2
 WIDTH = ACTIONS // HALVES
 PER_COLUMN = 16
+ROWS = 4
+PER_ROW = ACTIONS // ROWS
 WARM_UP = 14
 
 FLOPS = 2 * E * M * N + 2 * M * F * ACTIONS + 2 * F * ACTIONS
@@ -34,8 +36,8 @@ def tile_cardawarepolicy_kernel(tc, table, w, b1, w2, b2, w3, b3, offs, out):
         nc.sync.dma_start(b2_sb[:], b2)
         w3_sb = held.tile([F, 1], BF16, name="w3_sb")
         nc.scalar.dma_start(w3_sb[:], w3)
-        b3_sb = held.tile([1, 1], F32, name="b3_sb")
-        nc.sync.dma_start(b3_sb[:], b3)
+        b3_sb = held.tile([ROWS, 1], F32, name="b3_sb")
+        nc.sync.dma_start(b3_sb[:], b3.to_broadcast([ROWS, 1]))
 
         zeros = held.tile([128, 128], BF16, name="zeros")
         nc.vector.memset(zeros[:], 0.0)
@@ -47,6 +49,10 @@ def tile_cardawarepolicy_kernel(tc, table, w, b1, w2, b2, w3, b3, offs, out):
         nc.vector.tensor_scalar_mul(b1_x4[:], b1_sb[:], float(CARDS))
         b2_x4 = held.tile([F, 1], F32, name="b2_x4")
         nc.vector.tensor_scalar_mul(b2_x4[:], b2_sb[:], float(CARDS))
+
+        w3_spread = held.tile([F, ROWS * ROWS], BF16, name="w3_spread")
+        nc.vector.memset(w3_spread[:], 0.0)
+        nc.vector.tensor_copy(w3_spread[:, 0 : ROWS * ROWS : ROWS + 1], w3_sb[:].to_broadcast([F, ROWS]))
 
         sums = [psum.tile([M, WIDTH], F32, name=f"sums{h}") for h in range(HALVES)]
         for h in range(HALVES):
@@ -65,9 +71,16 @@ def tile_cardawarepolicy_kernel(tc, table, w, b1, w2, b2, w3, b3, offs, out):
             nc.tensor.matmul(layer2[h][:], w2_sb[:], h1_x4[h][:], start=True, stop=True)
             nc.vector.tensor_scalar(h2_x4[h][:], layer2[h][:], b2_x4[:], 0.0, ADD, MAX)
 
-        layer3 = [psum.tile([1, WIDTH], F32, name=f"layer3_{h}") for h in range(HALVES)]
-        scores = [held.tile([1, WIDTH], F32, name=f"scores{h}") for h in range(HALVES)]
-        for h in range(HALVES):
-            nc.tensor.matmul(layer3[h][:], w3_sb[:], h2_x4[h][:], start=True, stop=True)
-            nc.vector.tensor_scalar(scores[h][:], layer3[h][:], 1.0 / CARDS, b3_sb[:], MULT, ADD)
-            nc.sync.dma_start(out[:, h * WIDTH : (h + 1) * WIDTH], scores[h][:])
+        layer3 = psum.tile([ROWS, PER_ROW], F32, name="layer3")
+        for r in range(ROWS):
+            h, first = divmod(r * PER_ROW, WIDTH)
+            nc.tensor.matmul(
+                layer3[:],
+                w3_spread[:, r * ROWS : (r + 1) * ROWS],
+                h2_x4[h][:, first : first + PER_ROW],
+                start=(r == 0),
+                stop=(r == ROWS - 1),
+            )
+        scores = held.tile([ROWS, PER_ROW], F32, name="scores")
+        nc.vector.tensor_scalar(scores[:], layer3[:], 1.0 / CARDS, b3_sb[:], MULT, ADD)
+        nc.sync.dma_start(out.rearrange("o (r a) -> (o r) a", r=ROWS), scores[:])

@@ -6,8 +6,8 @@ MULT, ADD, MAX = mybir.AluOpType.mult, mybir.AluOpType.add, mybir.AluOpType.max
 E, S, M, F = 128, 512, 128, 128
 CARDS, ACTIONS = 4, 512
 N = CARDS * ACTIONS
-HALVES = 2
-WIDTH = ACTIONS // HALVES
+WIDTHS = (256, 128, 128)
+PIECES = tuple((sum(WIDTHS[:p]), WIDTHS[p]) for p in range(len(WIDTHS)))
 PER_COLUMN = 16
 ROWS = 4
 PER_ROW = ACTIONS // ROWS
@@ -54,33 +54,34 @@ def tile_cardawarepolicy_kernel(tc, table, w, b1, w2, b2, w3, b3, offs, out):
         nc.vector.memset(w3_spread[:], 0.0)
         nc.vector.tensor_copy(w3_spread[:, 0 : ROWS * ROWS : ROWS + 1], w3_sb[:].to_broadcast([F, ROWS]))
 
-        sums = [psum.tile([M, WIDTH], F32, name=f"sums{h}") for h in range(HALVES)]
-        for h in range(HALVES):
+        sums = [psum.tile([M, width], F32, name=f"sums{p}") for p, (first, width) in enumerate(PIECES)]
+        for p, (first, width) in enumerate(PIECES):
             for card in range(CARDS):
-                first = (card * ACTIONS + h * WIDTH) // PER_COLUMN
-                picked = cards[:].indirect(offsets[:, first : first + WIDTH // PER_COLUMN])
-                nc.tensor.matmul(sums[h][:], w_sb[:], picked, start=(card == 0), stop=(card == CARDS - 1))
+                column = (card * ACTIONS + first) // PER_COLUMN
+                picked = cards[:].indirect(offsets[:, column : column + width // PER_COLUMN])
+                nc.tensor.matmul(sums[p][:], w_sb[:], picked, start=(card == 0), stop=(card == CARDS - 1))
 
-        h1_x4 = [held.tile([M, WIDTH], BF16, name=f"h1_x4_{h}") for h in range(HALVES)]
-        for h in range(HALVES):
-            nc.vector.tensor_scalar(h1_x4[h][:], sums[h][:], b1_x4[:], 0.0, ADD, MAX)
+        h1_x4 = [held.tile([M, width], BF16, name=f"h1_x4_{p}") for p, (first, width) in enumerate(PIECES)]
+        for p in range(len(PIECES)):
+            nc.vector.tensor_scalar(h1_x4[p][:], sums[p][:], b1_x4[:], 0.0, ADD, MAX)
 
-        layer2 = [psum.tile([F, WIDTH], F32, name=f"layer2_{h}") for h in range(HALVES)]
-        h2_x4 = [held.tile([F, WIDTH], BF16, name=f"h2_x4_{h}") for h in range(HALVES)]
-        for h in range(HALVES):
-            nc.tensor.matmul(layer2[h][:], w2_sb[:], h1_x4[h][:], start=True, stop=True)
-            nc.vector.tensor_scalar(h2_x4[h][:], layer2[h][:], b2_x4[:], 0.0, ADD, MAX)
+        layer2 = [psum.tile([F, width], F32, name=f"layer2_{p}") for p, (first, width) in enumerate(PIECES)]
+        h2_x4 = [held.tile([F, width], BF16, name=f"h2_x4_{p}") for p, (first, width) in enumerate(PIECES)]
+        for p in range(len(PIECES)):
+            nc.tensor.matmul(layer2[p][:], w2_sb[:], h1_x4[p][:], start=True, stop=True)
+            nc.vector.tensor_scalar(h2_x4[p][:], layer2[p][:], b2_x4[:], 0.0, ADD, MAX)
 
         layer3 = psum.tile([ROWS, PER_ROW], F32, name="layer3")
-        for r in range(ROWS):
-            h, first = divmod(r * PER_ROW, WIDTH)
-            nc.tensor.matmul(
-                layer3[:],
-                w3_spread[:, r * ROWS : (r + 1) * ROWS],
-                h2_x4[h][:, first : first + PER_ROW],
-                start=(r == 0),
-                stop=(r == ROWS - 1),
-            )
+        for p, (first, width) in enumerate(PIECES):
+            for inside in range(0, width, PER_ROW):
+                r = (first + inside) // PER_ROW
+                nc.tensor.matmul(
+                    layer3[:],
+                    w3_spread[:, r * ROWS : (r + 1) * ROWS],
+                    h2_x4[p][:, inside : inside + PER_ROW],
+                    start=(r == 0),
+                    stop=(r == ROWS - 1),
+                )
         scores = held.tile([ROWS, PER_ROW], F32, name="scores")
         nc.vector.tensor_scalar(scores[:], layer3[:], 1.0 / CARDS, b3_sb[:], MULT, ADD)
         nc.sync.dma_start(out.rearrange("o (r a) -> (o r) a", r=ROWS), scores[:])

@@ -6,10 +6,10 @@ MULT, ADD, MAX = mybir.AluOpType.mult, mybir.AluOpType.add, mybir.AluOpType.max
 E, S, M, F = 128, 512, 128, 128
 CARDS, ACTIONS = 4, 512
 N = CARDS * ACTIONS
-WIDTHS = (256, 128, 128)
+WIDTHS = (256, 128, 64, 64)
 PIECES = tuple((sum(WIDTHS[:p]), WIDTHS[p]) for p in range(len(WIDTHS)))
 PER_COLUMN = 16
-ROWS = 4
+ROWS = 8
 PER_ROW = ACTIONS // ROWS
 WARM_UP = 14
 
@@ -54,7 +54,7 @@ def tile_cardawarepolicy_kernel(tc, table, w, b1, w2, b2, w3, b3, offs, out):
         nc.vector.memset(w3_spread[:], 0.0)
         nc.vector.tensor_copy(w3_spread[:, 0 : ROWS * ROWS : ROWS + 1], w3_sb[:].to_broadcast([F, ROWS]))
 
-        sums = [psum.tile([M, width], F32, name=f"sums{p}") for p, (first, width) in enumerate(PIECES)]
+        sums = [psum.tile([M, width], F32, name=f"sums{p}", tag=f"piece{p}") for p, (first, width) in enumerate(PIECES)]
         for p, (first, width) in enumerate(PIECES):
             for card in range(CARDS):
                 column = (card * ACTIONS + first) // PER_COLUMN
@@ -65,7 +65,7 @@ def tile_cardawarepolicy_kernel(tc, table, w, b1, w2, b2, w3, b3, offs, out):
         for p in range(len(PIECES)):
             nc.vector.tensor_scalar(h1_x4[p][:], sums[p][:], b1_x4[:], 0.0, ADD, MAX)
 
-        layer2 = [psum.tile([F, width], F32, name=f"layer2_{p}") for p, (first, width) in enumerate(PIECES)]
+        layer2 = [psum.tile([F, width], F32, name=f"layer2_{p}", tag=f"piece{p}") for p, (first, width) in enumerate(PIECES)]
         h2_x4 = [held.tile([F, width], BF16, name=f"h2_x4_{p}") for p, (first, width) in enumerate(PIECES)]
         for p in range(len(PIECES)):
             nc.tensor.matmul(layer2[p][:], w2_sb[:], h1_x4[p][:], start=True, stop=True)

@@ -37,7 +37,7 @@ def tile_cardawarepolicy_kernel(tc, table, w, b1, w2, b2, w3, b3, offs, out):
         w3_sb = held.tile([F, 1], BF16, name="w3_sb")
         nc.scalar.dma_start(w3_sb[:], w3)
         b3_sb = held.tile([ROWS, 1], F32, name="b3_sb")
-        nc.sync.dma_start(b3_sb[:], b3.to_broadcast([ROWS, 1]))
+        nc.gpsimd.dma_start(b3_sb[:], b3.to_broadcast([ROWS, 1]))
 
         zeros = held.tile([128, 128], BF16, name="zeros")
         nc.vector.memset(zeros[:], 0.0)

@@ -11,7 +11,7 @@ PIECES = tuple((sum(WIDTHS[:p]), WIDTHS[p]) for p in range(len(WIDTHS)))
 PER_COLUMN = 16
 ROWS = 8
 PER_ROW = ACTIONS // ROWS
-WARM_UP = 14
+WARM_UP = 11
 
 FLOPS = 2 * E * M * N + 2 * M * F * ACTIONS + 2 * F * ACTIONS
 

@@ -36,8 +36,8 @@ def tile_cardawarepolicy_kernel(tc, table, w, b1, w2, b2, w3, b3, offs, out):
         nc.sync.dma_start(b2_sb[:], b2)
         w3_sb = held.tile([F, 1], BF16, name="w3_sb")
         nc.scalar.dma_start(w3_sb[:], w3)
-        b3_sb = held.tile([ROWS, 1], F32, name="b3_sb")
-        nc.gpsimd.dma_start(b3_sb[:], b3.to_broadcast([ROWS, 1]))
+        b3_sb = held.tile([1, 1], F32, name="b3_sb")
+        nc.gpsimd.dma_start(b3_sb[:], b3)
 
         zeros = held.tile([128, 128], BF16, name="zeros")
         nc.vector.memset(zeros[:], 0.0)
@@ -53,6 +53,12 @@ def tile_cardawarepolicy_kernel(tc, table, w, b1, w2, b2, w3, b3, offs, out):
         w3_spread = held.tile([F, ROWS * ROWS], BF16, name="w3_spread")
         nc.vector.memset(w3_spread[:], 0.0)
         nc.vector.tensor_copy(w3_spread[:, 0 : ROWS * ROWS : ROWS + 1], w3_sb[:].to_broadcast([F, ROWS]))
+
+        b3_row = held.tile([128, ROWS], F32, name="b3_row")
+        nc.gpsimd.memset(b3_row[:], 0.0)
+        nc.gpsimd.tensor_scalar(b3_row[0:1, :], b3_sb[:].to_broadcast([1, ROWS]), float(CARDS), None, MULT)
+        ones = held.tile([128, PER_ROW], F32, name="ones")
+        nc.gpsimd.memset(ones[:], 1.0)
 
         sums = [psum.tile([M, width], F32, name=f"sums{p}", tag=f"piece{p}") for p, (first, width) in enumerate(PIECES)]
         for p, (first, width) in enumerate(PIECES):
@@ -72,6 +78,7 @@ def tile_cardawarepolicy_kernel(tc, table, w, b1, w2, b2, w3, b3, offs, out):
             nc.vector.tensor_scalar(h2_x4[p][:], layer2[p][:], b2_x4[:], 0.0, ADD, MAX)
 
         layer3 = psum.tile([ROWS, PER_ROW], F32, name="layer3")
+        nc.tensor.matmul(layer3[:], b3_row[:], ones[:], start=True, stop=False)
         for p, (first, width) in enumerate(PIECES):
             for inside in range(0, width, PER_ROW):
                 r = (first + inside) // PER_ROW
@@ -79,9 +86,9 @@ def tile_cardawarepolicy_kernel(tc, table, w, b1, w2, b2, w3, b3, offs, out):
                     layer3[:],
                     w3_spread[:, r * ROWS : (r + 1) * ROWS],
                     h2_x4[p][:, inside : inside + PER_ROW],
-                    start=(r == 0),
+                    start=False,
                     stop=(r == ROWS - 1),
                 )
         scores = held.tile([ROWS, PER_ROW], F32, name="scores")
-        nc.vector.tensor_scalar(scores[:], layer3[:], 1.0 / CARDS, b3_sb[:], MULT, ADD)
+        nc.vector.tensor_scalar_mul(scores[:], layer3[:], 1.0 / CARDS)
         nc.sync.dma_start(out.rearrange("o (r a) -> (o r) a", r=ROWS), scores[:])

@@ -11,6 +11,7 @@ PIECES = tuple((sum(WIDTHS[:p]), WIDTHS[p]) for p in range(len(WIDTHS)))
 PER_COLUMN = 16
 ROWS = 8
 PER_ROW = ACTIONS // ROWS
+GROUP = 32
 WARM_UP = 11
 
 FLOPS = 2 * E * M * N + 2 * M * F * ACTIONS + 2 * F * ACTIONS
@@ -28,14 +29,15 @@ def tile_cardawarepolicy_kernel(tc, table, w, b1, w2, b2, w3, b3, offs, out):
         nc.scalar.dma_start(cards[:], table)
         w_sb = held.tile([E, M], BF16, name="w_sb")
         nc.sync.dma_start(w_sb[:], w)
-        b1_sb = held.tile([M, 1], F32, name="b1_sb")
-        nc.sync.dma_start(b1_sb[:], b1)
         w2_sb = held.tile([M, F], BF16, name="w2_sb")
         nc.scalar.dma_start(w2_sb[:], w2)
-        b2_sb = held.tile([F, 1], F32, name="b2_sb")
-        nc.sync.dma_start(b2_sb[:], b2)
-        w3_sb = held.tile([F, 1], BF16, name="w3_sb")
-        nc.scalar.dma_start(w3_sb[:], w3)
+        bias_rows = held.tile([128, GROUP], F32, name="bias_rows", align_bytes=64)
+        nc.vector.memset(bias_rows[:], 0.0)
+        nc.sync.dma_start(bias_rows[0:128:GROUP, :], b1.rearrange("(g c) o -> g (c o)", c=GROUP))
+        nc.sync.dma_start(bias_rows[1:128:GROUP, :], b2.rearrange("(g c) o -> g (c o)", c=GROUP))
+        w3_rows = held.tile([128, GROUP], BF16, name="w3_rows", align_bytes=64)
+        nc.vector.memset(w3_rows[:], 0.0)
+        nc.scalar.dma_start(w3_rows[0:128:GROUP, :], w3.rearrange("(g c) o -> g (c o)", c=GROUP))
         b3_sb = held.tile([1, 1], F32, name="b3_sb")
         nc.gpsimd.dma_start(b3_sb[:], b3)
 
@@ -45,14 +47,17 @@ def tile_cardawarepolicy_kernel(tc, table, w, b1, w2, b2, w3, b3, offs, out):
         for step in range(WARM_UP):
             nc.tensor.matmul(unread[:], zeros[:], zeros[:], start=True, stop=True)
 
-        b1_x4 = held.tile([M, 1], F32, name="b1_x4")
-        nc.vector.tensor_scalar_mul(b1_x4[:], b1_sb[:], float(CARDS))
-        b2_x4 = held.tile([F, 1], F32, name="b2_x4")
-        nc.vector.tensor_scalar_mul(b2_x4[:], b2_sb[:], float(CARDS))
+        bias_columns = held.tile([128, GROUP], F32, name="bias_columns", align_bytes=64)
+        nc.vector.transpose(bias_columns[:], bias_rows[:])
+        biases_x4 = held.tile([128, 2], F32, name="biases_x4")
+        nc.vector.tensor_scalar_mul(biases_x4[:], bias_columns[:, 0:2], float(CARDS))
+        b1_x4, b2_x4 = biases_x4[:, 0:1], biases_x4[:, 1:2]
 
+        w3_columns = held.tile([128, GROUP], BF16, name="w3_columns", align_bytes=64)
+        nc.vector.transpose(w3_columns[:], w3_rows[:])
         w3_spread = held.tile([F, ROWS * ROWS], BF16, name="w3_spread")
         nc.vector.memset(w3_spread[:], 0.0)
-        nc.vector.tensor_copy(w3_spread[:, 0 : ROWS * ROWS : ROWS + 1], w3_sb[:].to_broadcast([F, ROWS]))
+        nc.vector.tensor_copy(w3_spread[:, 0 : ROWS * ROWS : ROWS + 1], w3_columns[:, 0:1].to_broadcast([F, ROWS]))
 
         b3_row = held.tile([128, ROWS], F32, name="b3_row")
         nc.gpsimd.memset(b3_row[:], 0.0)
@@ -69,13 +74,13 @@ def tile_cardawarepolicy_kernel(tc, table, w, b1, w2, b2, w3, b3, offs, out):
 
         h1_x4 = [held.tile([M, width], BF16, name=f"h1_x4_{p}") for p, (first, width) in enumerate(PIECES)]
         for p in range(len(PIECES)):
-            nc.vector.tensor_scalar(h1_x4[p][:], sums[p][:], b1_x4[:], 0.0, ADD, MAX)
+            nc.vector.tensor_scalar(h1_x4[p][:], sums[p][:], b1_x4, 0.0, ADD, MAX)
 
         layer2 = [psum.tile([F, width], F32, name=f"layer2_{p}", tag=f"piece{p}") for p, (first, width) in enumerate(PIECES)]
         h2_x4 = [held.tile([F, width], BF16, name=f"h2_x4_{p}") for p, (first, width) in enumerate(PIECES)]
         for p in range(len(PIECES)):
             nc.tensor.matmul(layer2[p][:], w2_sb[:], h1_x4[p][:], start=True, stop=True)
-            nc.vector.tensor_scalar(h2_x4[p][:], layer2[p][:], b2_x4[:], 0.0, ADD, MAX)
+            nc.vector.tensor_scalar(h2_x4[p][:], layer2[p][:], b2_x4, 0.0, ADD, MAX)
 
         layer3 = psum.tile([ROWS, PER_ROW], F32, name="layer3")
         nc.tensor.matmul(layer3[:], b3_row[:], ones[:], start=True, stop=False)

@@ -66,11 +66,14 @@ def tile_cardawarepolicy_kernel(tc, table, w, b1, w2, b2, w3, b3, offs, out):
         nc.gpsimd.memset(ones[:], 1.0)
 
         sums = [psum.tile([M, width], F32, name=f"sums{p}", tag=f"piece{p}") for p, (first, width) in enumerate(PIECES)]
-        for p, (first, width) in enumerate(PIECES):
-            for card in range(CARDS):
-                column = (card * ACTIONS + first) // PER_COLUMN
-                picked = cards[:].indirect(offsets[:, column : column + width // PER_COLUMN])
-                nc.tensor.matmul(sums[p][:], w_sb[:], picked, start=(card == 0), stop=(card == CARDS - 1))
+        for pair in range(0, len(PIECES), 2):
+            for turn in range(CARDS + 2):
+                for p, card in ((pair, turn), (pair + 1, turn - 2)):
+                    if 0 <= card < CARDS:
+                        first, width = PIECES[p]
+                        column = (card * ACTIONS + first) // PER_COLUMN
+                        picked = cards[:].indirect(offsets[:, column : column + width // PER_COLUMN])
+                        nc.tensor.matmul(sums[p][:], w_sb[:], picked, start=(card == 0), stop=(card == CARDS - 1))
 
         h1_x4 = [held.tile([M, width], BF16, name=f"h1_x4_{p}") for p, (first, width) in enumerate(PIECES)]
         for p in range(len(PIECES)):

import concourse.mybir as mybir

BF16, F32, U16 = mybir.dt.bfloat16, mybir.dt.float32, mybir.dt.uint16
MULT, ADD, MAX = mybir.AluOpType.mult, mybir.AluOpType.add, mybir.AluOpType.max

E, S, M, F = 128, 512, 128, 128
CARDS, ACTIONS = 4, 512
N = CARDS * ACTIONS
WIDTHS = (256, 128, 64, 64)
PIECES = tuple((sum(WIDTHS[:p]), WIDTHS[p]) for p in range(len(WIDTHS)))
PER_COLUMN = 16
ROWS = 8
PER_ROW = ACTIONS // ROWS
GROUP = 32
WARM_UP = 11

FLOPS = 2 * E * M * N + 2 * M * F * ACTIONS + 2 * F * ACTIONS


def tile_cardawarepolicy_kernel(tc, table, w, b1, w2, b2, w3, b3, offs, out):
    nc = tc.nc
    with (
        tc.tile_pool(name="held", bufs=1) as held,
        tc.psum_pool(name="psum", bufs=1) as psum,
    ):
        offsets = held.tile([128, N // PER_COLUMN], U16, name="offsets")
        nc.sync.dma_start(offsets[:], offs)
        cards = held.tile([E, S], BF16, name="cards")
        nc.scalar.dma_start(cards[:], table)
        w_sb = held.tile([E, M], BF16, name="w_sb")
        nc.sync.dma_start(w_sb[:], w)
        w2_sb = held.tile([M, F], BF16, name="w2_sb")
        nc.scalar.dma_start(w2_sb[:], w2)
        bias_rows = held.tile([128, GROUP], F32, name="bias_rows", align_bytes=64)
        nc.vector.memset(bias_rows[:], 0.0)
        nc.sync.dma_start(bias_rows[0:128:GROUP, :], b1.rearrange("(g c) o -> g (c o)", c=GROUP))
        nc.sync.dma_start(bias_rows[1:128:GROUP, :], b2.rearrange("(g c) o -> g (c o)", c=GROUP))
        w3_rows = held.tile([128, GROUP], BF16, name="w3_rows", align_bytes=64)
        nc.vector.memset(w3_rows[:], 0.0)
        nc.scalar.dma_start(w3_rows[0:128:GROUP, :], w3.rearrange("(g c) o -> g (c o)", c=GROUP))
        b3_sb = held.tile([1, 1], F32, name="b3_sb")
        nc.gpsimd.dma_start(b3_sb[:], b3)

        zeros = held.tile([128, 128], BF16, name="zeros")
        nc.vector.memset(zeros[:], 0.0)
        unread = psum.tile([128, 128], F32, name="unread")
        for step in range(WARM_UP):
            nc.tensor.matmul(unread[:], zeros[:], zeros[:], start=True, stop=True)

        bias_columns = held.tile([128, GROUP], F32, name="bias_columns", align_bytes=64)
        nc.vector.transpose(bias_columns[:], bias_rows[:])
        biases_x4 = held.tile([128, 2], F32, name="biases_x4")
        nc.vector.tensor_scalar_mul(biases_x4[:], bias_columns[:, 0:2], float(CARDS))
        b1_x4, b2_x4 = biases_x4[:, 0:1], biases_x4[:, 1:2]

        w3_columns = held.tile([128, GROUP], BF16, name="w3_columns", align_bytes=64)
        nc.vector.transpose(w3_columns[:], w3_rows[:])
        w3_spread = held.tile([F, ROWS * ROWS], BF16, name="w3_spread")
        nc.vector.memset(w3_spread[:], 0.0)
        nc.vector.tensor_copy(w3_spread[:, 0 : ROWS * ROWS : ROWS + 1], w3_columns[:, 0:1].to_broadcast([F, ROWS]))

        b3_row = held.tile([128, ROWS], F32, name="b3_row")
        nc.gpsimd.memset(b3_row[:], 0.0)
        nc.gpsimd.tensor_scalar(b3_row[0:1, :], b3_sb[:].to_broadcast([1, ROWS]), float(CARDS), None, MULT)
        ones = held.tile([128, PER_ROW], F32, name="ones")
        nc.gpsimd.memset(ones[:], 1.0)

        sums = [psum.tile([M, width], F32, name=f"sums{p}", tag=f"piece{p}") for p, (first, width) in enumerate(PIECES)]
        for pair in range(0, len(PIECES), 2):
            for turn in range(CARDS + 2):
                for p, card in ((pair, turn), (pair + 1, turn - 2)):
                    if 0 <= card < CARDS:
                        first, width = PIECES[p]
                        column = (card * ACTIONS + first) // PER_COLUMN
                        picked = cards[:].indirect(offsets[:, column : column + width // PER_COLUMN])
                        nc.tensor.matmul(sums[p][:], w_sb[:], picked, start=(card == 0), stop=(card == CARDS - 1))

        h1_x4 = [held.tile([M, width], BF16, name=f"h1_x4_{p}") for p, (first, width) in enumerate(PIECES)]
        for p in range(len(PIECES)):
            nc.vector.tensor_scalar(h1_x4[p][:], sums[p][:], b1_x4, 0.0, ADD, MAX)

        layer2 = [psum.tile([F, width], F32, name=f"layer2_{p}", tag=f"piece{p}") for p, (first, width) in enumerate(PIECES)]
        h2_x4 = [held.tile([F, width], BF16, name=f"h2_x4_{p}") for p, (first, width) in enumerate(PIECES)]
        for p in range(len(PIECES)):
            nc.tensor.matmul(layer2[p][:], w2_sb[:], h1_x4[p][:], start=True, stop=True)
            nc.vector.tensor_scalar(h2_x4[p][:], layer2[p][:], b2_x4, 0.0, ADD, MAX)

        layer3 = psum.tile([ROWS, PER_ROW], F32, name="layer3")
        nc.tensor.matmul(layer3[:], b3_row[:], ones[:], start=True, stop=False)
        for p, (first, width) in enumerate(PIECES):
            for inside in range(0, width, PER_ROW):
                r = (first + inside) // PER_ROW
                nc.tensor.matmul(
                    layer3[:],
                    w3_spread[:, r * ROWS : (r + 1) * ROWS],
                    h2_x4[p][:, inside : inside + PER_ROW],
                    start=False,
                    stop=(r == ROWS - 1),
                )
        scores = held.tile([ROWS, PER_ROW], F32, name="scores")
        nc.vector.tensor_scalar_mul(scores[:], layer3[:], 1.0 / CARDS)
        nc.sync.dma_start(out.rearrange("o (r a) -> (o r) a", r=ROWS), scores[:])
